import numpy as np
import ml_dtypes


def mxq(x, axis, fmt="e4m3"):
    dtype, down = {"e4m3": (ml_dtypes.float8_e4m3fn, 7), "e5m2": (ml_dtypes.float8_e5m2, 14)}[fmt]
    v = np.moveaxis(np.asarray(x, np.float32).astype(ml_dtypes.bfloat16).astype(np.float64), axis, -1)
    blocks = v.reshape(v.shape[:-1] + (-1, 32))
    amax = np.abs(blocks).max(-1, keepdims=True)
    byte = np.maximum(np.where(amax > 0, np.frexp(amax)[1] - 1 + 127, 0) - down, 1)
    scale = np.exp2(byte - 127.0)
    codes = (blocks / scale).astype(np.float32).astype(dtype).astype(np.float64)
    return np.moveaxis((codes * scale).reshape(v.shape), -1, axis)


WIDE = False


def mx_kscale(k):
    if not WIDE:
        return np.ones(k)
    levels = np.array([10, -10, 5, -5, 0])
    a = np.random.permutation(np.resize(levels, k // 512 * 4)).reshape(k // 512, 4)
    idx = np.arange(k)
    return np.exp2(a[idx // 512, idx % 128 // 32])


BF16 = ml_dtypes.bfloat16


def bf(x):
    return np.asarray(x, np.float32).astype(BF16)


def f64(x):
    return np.asarray(x).astype(np.float64)


B, N, S, D = 32, 512, 1024, 128
G = 8
BLK = 32
LERP_MEAN = 1.0986122886681098


def sigmoid(v):
    return 1.0 / (1.0 + np.exp(-v))


def setup_inputs():
    c = np.random.standard_normal((G, D))
    r = np.random.uniform(0.1, 0.6, (S, 1))
    data = c[np.random.randint(0, G, S)] + r * np.random.standard_normal((S, D))
    node_fts = c[np.random.randint(0, G, (B, N))] + 0.25 * np.random.standard_normal((B, N, D))
    k = mx_kscale(S)
    L = k.max() / k.min()
    alt = np.where(np.arange(BLK) % 2 == 0, 1.0, -1.0)[:, None]
    data[:BLK] = data[:BLK] + (L - 1.0) * alt
    return {"node_fts": bf(node_fts), "data": bf(data),
            "temp": bf((1.0 + 0.1 * np.random.standard_normal(1)) * 1.5 / np.sqrt(D)),
            "fixed_lerp": bf(LERP_MEAN + 0.1 * np.random.standard_normal(1))}


def reference(node_fts, data, temp, fixed_lerp):
    q, m = f64(node_fts), f64(data)
    q2 = np.sum(q * q, axis=-1)
    m2 = np.sum(m * m, axis=-1)
    cross = q @ m.T
    d2 = q2[..., None] + m2[None, None, :] - 2.0 * cross
    ds = np.sqrt(np.maximum(d2, 1e-12))
    s = np.exp(-f64(temp) * ds)
    e = np.exp(s - s.max(-1, keepdims=True))
    data_goal = (mxq(e, 2, "e4m3") @ mxq(m, 0, "e4m3")) / e.sum(-1, keepdims=True)
    lerp = sigmoid(f64(fixed_lerp))
    return lerp * data_goal + (1.0 - lerp) * q

@@ -1,0 +1,372 @@
+from contextlib import ExitStack
+
+import concourse.mybir as mybir
+from concourse.masks import make_identity
+
+F32 = mybir.dt.float32
+BF16 = mybir.dt.bfloat16
+U32 = mybir.dt.uint32
+U8 = mybir.dt.uint8
+FP8X4 = mybir.dt.float8_e4m3fn_x4
+ALU = mybir.AluOpType
+FN = mybir.ActivationFunctionType
+AX = mybir.AxisListType
+
+P = 128
+NODES = 32 * 512
+S = 1024
+D = 128
+NT = NODES // P
+HALF = 512
+EPS = 1e-12
+FLOPS = 2 * NODES * S * D * 2
+
+BATCHES = [12, 20, 32, 32, 32]
+RING = 32
+AHEAD = [8, 14, 22, 22, 0]
+
+
+def tile_pernodememory_t_kernel(tc, node_fts, data, temp, fixed_lerp, out):
+    nc = tc.nc
+    qv = node_fts.flatten_outer_dims().rearrange("(p t) d -> p t d", t=NT)
+    ov = out.flatten_outer_dims().rearrange("(p t) d -> p t d", t=NT)
+
+    starts = [sum(BATCHES[:b]) for b in range(len(BATCHES))]
+    batch_of = []
+    for b in range(len(BATCHES)):
+        batch_of.extend([b] * BATCHES[b])
+
+    with ExitStack() as ctx:
+        const = ctx.enter_context(tc.tile_pool(name="const", bufs=1))
+        ring = ctx.enter_context(tc.tile_pool(name="ring", bufs=RING))
+        epool = ctx.enter_context(tc.tile_pool(name="epool", bufs=4))
+        grpool = ctx.enter_context(tc.tile_pool(name="grpool", bufs=3))
+        cdpool = ctx.enter_context(tc.tile_pool(name="cdpool", bufs=8))
+        qtpool = ctx.enter_context(tc.tile_pool(name="qtpool", bufs=10))
+        sqpool = ctx.enter_context(tc.tile_pool(name="sqpool", bufs=2))
+        qspool = ctx.enter_context(tc.tile_pool(name="qspool", bufs=2))
+        obpool = ctx.enter_context(tc.tile_pool(name="obpool", bufs=3))
+        small = ctx.enter_context(tc.tile_pool(name="small", bufs=2))
+        psx = ctx.enter_context(tc.psum_pool(name="psx", bufs=4))
+        pse = ctx.enter_context(tc.psum_pool(name="pse", bufs=2))
+        psg = ctx.enter_context(tc.psum_pool(name="psg", bufs=1))
+        psq = ctx.enter_context(tc.psum_pool(name="psq", bufs=1))
+        ctx.enter_context(tc.manual_schedule())
+
+        dk = const.tile([P, 2, 4, D], BF16)
+        nc.sync.dma_start(out=dk[:], in_=data.rearrange("(g p t) d -> p g t d", g=2, t=4))
+        q_sb = const.tile([P, NT, D], BF16)
+        nc.sync.dma_start(out=q_sb[:, 0 : BATCHES[0], :], in_=qv[:, 0 : BATCHES[0], :])
+        lerp_bf = const.tile([P, 1], BF16)
+        nc.scalar.dma_start(out=lerp_bf[:], in_=fixed_lerp.partition_broadcast(P))
+        temp_bf = const.tile([P, 1], BF16)
+        nc.scalar.dma_start(out=temp_bf[:], in_=temp.partition_broadcast(P))
+        for b in range(1, len(BATCHES)):
+            t0 = starts[b]
+            t1 = t0 + BATCHES[b]
+            nc.sync.dma_start(out=q_sb[:, t0:t1, :], in_=qv[:, t0:t1, :])
+
+        ident_b = const.tile([P, P], BF16)
+        make_identity(nc, ident_b[:])
+        ident_f = const.tile([P, P], F32)
+        make_identity(nc, ident_f[:])
+
+        z = const.tile([P, 1], F32)
+        nc.scalar.activation(out=z[:], in_=lerp_bf[:], func=FN.Exp, scale=-1.0)
+        m2col = const.tile([P, 8], F32)
+        junk = const.tile([P, D], F32)
+        for i in range(8):
+            nc.scalar.activation(
+                out=junk[:], in_=dk[:, i // 4, i % 4, :], func=FN.Square, accum_out=m2col[:, i : i + 1]
+            )
+        warm = const.tile([P, 1], F32)
+        nc.scalar.activation(out=warm[:], in_=z[:], func=FN.Sqrt)
+
+        mt_ps = psq.tile([P, 8, P], BF16, tag="qt")
+        for i in range(8):
+            nc.tensor.transpose(mt_ps[:, i, :], dk[:, i // 4, i % 4, :], ident_b[:])
+        mT2 = const.tile([D, S], BF16)
+        nc.vector.tensor_scalar(
+            out=mT2[:],
+            in0=mt_ps[:].rearrange("d i p -> d (i p)"),
+            scalar1=-2.0,
+            scalar2=None,
+            op0=ALU.mult,
+        )
+
+        ntemp = const.tile([P, 1], F32)
+        lerp = const.tile([P, 1], F32)
+        oml = const.tile([P, 1], F32)
+        dcodes = const.tile([P, 2 * D], U32, align_bytes=64)
+        dscales = const.tile([P, 2 * D], U8, align_bytes=64)
+
+        def small_constants():
+            nc.vector.tensor_scalar(
+                out=ntemp[:], in0=temp_bf[:], scalar1=-1.0, scalar2=None, op0=ALU.mult
+            )
+            den = const.tile([P, 1], F32)
+            nc.vector.tensor_scalar(out=den[:], in0=z[:], scalar1=1.0, scalar2=None, op0=ALU.add)
+            nc.vector.reciprocal(out=lerp[:], in_=den[:])
+            nc.vector.tensor_tensor(out=oml[:], in0=z[:], in1=lerp[:], op=ALU.mult)
+
+        def quantise_data():
+            dg = const.tile([P, 2, D, 4], BF16, align_bytes=64)
+            nc.vector.tensor_copy(out=dg[:], in_=dk[:].rearrange("p g t d -> p g d t"))
+            nc.vector.quantize_mx(
+                out=dcodes[:].bitcast(FP8X4),
+                scales=dscales[:],
+                in_=dg[:].rearrange("p g d t -> p (g d t)"),
+            )
+
+        qT = {}
+        q2b = {}
+        cb = {}
+        umin = {}
+        nmx = {}
+        rs = {}
+        xs = {}
+        us = {}
+        es = {}
+        ets = {}
+        grs = {}
+        cds = {}
+        gps = {}
+        qss = {}
+        done = {"prep": 0, "cross": 0, "clamp": 0}
+
+        def where(i):
+            b = batch_of[i]
+            return b, i - starts[b]
+
+        def prep(quad):
+            i0 = 4 * quad
+            b, k0 = where(i0)
+            if k0 == 0:
+                q2_t = small.tile([P, RING], F32, tag="q2b")
+                q2b[b] = q2_t
+                c_t = small.tile([P, RING], F32, tag="cb")
+                cb[b] = c_t
+            qt_ps = psq.tile([P, 4, P], BF16, tag="qt")
+            for k in range(4):
+                nc.tensor.transpose(qt_ps[:, k, :], q_sb[:, i0 + k, :], ident_b[:])
+            qt_sb = qtpool.tile([D, 4, P], BF16, tag="qT")
+            nc.vector.tensor_copy(out=qt_sb[:], in_=qt_ps[:])
+            qT[quad] = qt_sb
+            sq = sqpool.tile([P, 4, D], F32, tag="sq")
+            nc.gpsimd.tensor_tensor(
+                out=sq[:], in0=q_sb[:, i0 : i0 + 4, :], in1=q_sb[:, i0 : i0 + 4, :], op=ALU.mult
+            )
+            nc.vector.tensor_reduce(out=q2b[b][:, k0 : k0 + 4], in_=sq[:], axis=AX.X, op=ALU.add)
+            nc.vector.tensor_scalar(
+                out=cb[b][:, k0 : k0 + 4],
+                in0=q2b[b][:, k0 : k0 + 4],
+                scalar1=-1.0,
+                scalar2=EPS,
+                op0=ALU.mult,
+                op1=ALU.add,
+            )
+            done["prep"] = quad + 1
+
+        def cross(i):
+            banks = []
+            for h in range(2):
+                x = psx.tile([P, HALF], F32, tag="x")
+                nc.tensor.matmul(
+                    out=x[:],
+                    lhsT=qT[i // 4][:, i % 4, :],
+                    rhs=mT2[:, HALF * h : HALF * (h + 1)],
+                    start=True,
+                    stop=False,
+                )
+                for a in range(4):
+                    c = 4 * h + a
+                    nc.tensor.matmul(
+                        out=x[:, P * a : P * (a + 1)],
+                        lhsT=m2col[:, c : c + 1].to_broadcast([P, P]),
+                        rhs=ident_f[:],
+                        is_transpose=True,
+                        start=False,
+                        stop=(a == 3),
+                    )
+                banks.append(x)
+            xs[i] = banks
+            done["cross"] = i + 1
+
+        def clamp(i):
+            b, k = where(i)
+            if k == 0:
+                um = small.tile([P, RING, 2], F32, tag="umin")
+                umin[b] = um
+            u = ring.tile([P, S], F32, tag="u")
+            for h in range(2):
+                nc.vector.tensor_scalar(
+                    out=u[:, HALF * h : HALF * (h + 1)],
+                    in0=xs[i][h][:],
+                    scalar1=cb[b][:, k : k + 1],
+                    scalar2=None,
+                    op0=ALU.max,
+                    op1=ALU.min,
+                    accum_out=umin[b][:, k, h : h + 1],
+                )
+            us[i] = u
+            done["clamp"] = i + 1
+
+        def produce():
+            i = done["clamp"]
+            for j in (i, i + 1):
+                if j == done["cross"] and j < NT and j // 4 < done["prep"]:
+                    cross(j)
+            clamp(i)
+
+        def root(i):
+            b, k = where(i)
+            nc.scalar.activation(
+                out=us[i][:], in_=us[i][:], func=FN.Sqrt, bias=q2b[b][:, k : k + 1], scale=1.0
+            )
+
+        def exp1(i):
+            nc.scalar.activation(out=us[i][:], in_=us[i][:], func=FN.Exp, scale=ntemp[:, 0:1])
+
+        def exp2(i):
+            b, k = where(i)
+            e = epool.tile([P, S], BF16, tag="e")
+            nc.scalar.activation(
+                out=e[:],
+                in_=us[i][:],
+                func=FN.Exp,
+                bias=nmx[b][:, k : k + 1],
+                scale=1.0,
+                accum_out=rs[b][:, k : k + 1],
+            )
+            es[i] = e
+
+        def flip(i):
+            et = pse.tile([P, 8, P], BF16, tag="et")
+            for c in range(8):
+                nc.tensor.transpose(et[:, c, :], es[i][:, P * c : P * (c + 1)], ident_b[:])
+            ets[i] = et
+
+        def regroup(i):
+            gr = grpool.tile([P, S], BF16, tag="gr", align_bytes=64)
+            nc.vector.tensor_copy(
+                out=gr[:].rearrange("p (g n t) -> p g n t", g=2, t=4),
+                in_=ets[i][:].rearrange("p (g t) n -> p g n t", t=4),
+            )
+            grs[i] = gr
+
+        def quant(i):
+            codes = cdpool.tile([P, 2 * P], U32, tag="codes", align_bytes=64)
+            scales = cdpool.tile([P, 2 * P], U8, tag="scales", align_bytes=64)
+            nc.vector.quantize_mx(out=codes[:].bitcast(FP8X4), scales=scales[:], in_=grs[i][:])
+            cds[i] = (codes, scales)
+
+        def read_memory(quad):
+            gp = psg.tile([P, 4, D], F32, tag="g")
+            for k in range(4):
+                codes, scales = cds[4 * quad + k]
+                for g in range(2):
+                    nc.tensor.matmul_mx(
+                        out=gp[:, k, :],
+                        lhsT=codes[:, P * g : P * (g + 1)].bitcast(FP8X4),
+                        lhsT_scale=scales[:, P * g : P * (g + 1)],
+                        rhs=dcodes[:, D * g : D * (g + 1)].bitcast(FP8X4),
+                        rhs_scale=dscales[:, D * g : D * (g + 1)],
+                        start=(g == 0),
+                        stop=(g == 1),
+                    )
+            gps[quad] = gp
+
+        def scale_q(quad):
+            qs = qspool.tile([P, 4, D], F32, tag="qs")
+            nc.gpsimd.tensor_scalar(
+                out=qs[:],
+                in0=q_sb[:, 4 * quad : 4 * quad + 4, :],
+                scalar1=oml[:, 0:1],
+                scalar2=0.0,
+                op0=ALU.mult,
+                op1=ALU.add,
+            )
+            qss[quad] = qs
+
+        def finish(quad):
+            b, k0 = where(4 * quad)
+            ra = small.tile([P, 4], F32, tag="ra")
+            nc.vector.reciprocal(out=ra[:], in_=rs[b][:, k0 : k0 + 4])
+            wgt = small.tile([P, 4], F32, tag="wgt")
+            nc.vector.tensor_scalar(
+                out=wgt[:], in0=ra[:], scalar1=lerp[:, 0:1], scalar2=None, op0=ALU.mult
+            )
+            ob = obpool.tile([P, 4, D], F32, tag="ob")
+            for k in range(4):
+                nc.vector.scalar_tensor_tensor(
+                    out=ob[:, k, :],
+                    in0=gps[quad][:, k, :],
+                    scalar=wgt[:, k : k + 1],
+                    in1=qss[quad][:, k, :],
+                    op0=ALU.mult,
+                    op1=ALU.add,
+                )
+            nc.sync.dma_start(out=ov[:, 4 * quad : 4 * quad + 4, :], in_=ob[:])
+
+        def consume(b, step):
+            i0 = starts[b]
+            n = BATCHES[b]
+            if 0 <= step - 1 < n:
+                flip(i0 + step - 1)
+            if step >= 6 and (step - 6) % 4 == 0 and step - 6 < n:
+                read_memory((i0 + step - 6) // 4)
+            if step >= 3 and (step - 3) % 4 == 0 and step - 3 < n:
+                scale_q((i0 + step - 3) // 4)
+            if 0 <= step - 1 < n:
+                regroup(i0 + step - 1)
+            if 0 <= step - 2 < n:
+                quant(i0 + step - 2)
+            if step >= 7 and (step - 7) % 4 == 0 and step - 7 < n:
+                finish((i0 + step - 7) // 4)
+
+        for quad in range(BATCHES[0] // 4):
+            prep(quad)
+
+        for b in range(len(BATCHES)):
+            i0 = starts[b]
+            n = BATCHES[b]
+            if b > 0:
+                for step in range(BATCHES[b - 1], BATCHES[b - 1] + 8):
+                    consume(b - 1, step)
+            while done["clamp"] < i0 + n:
+                produce()
+            dmin = small.tile([P, RING], F32, tag="dmin")
+            nc.vector.tensor_reduce(out=dmin[:, 0:n], in_=umin[b][:, 0:n, :], axis=AX.X, op=ALU.min)
+            nc.vector.tensor_tensor(
+                out=dmin[:, 0:n], in0=dmin[:, 0:n], in1=q2b[b][:, 0:n], op=ALU.add
+            )
+            if b == 0:
+                small_constants()
+                quantise_data()
+            if b + 1 < len(BATCHES):
+                for quad in range(starts[b + 1] // 4, (starts[b + 1] + BATCHES[b + 1]) // 4):
+                    prep(quad)
+            for k in range(n):
+                root(i0 + k)
+            nc.scalar.activation(out=dmin[:, 0:n], in_=dmin[:, 0:n], func=FN.Sqrt)
+            mx = small.tile([P, RING], F32, tag="mx")
+            nc.scalar.activation(out=mx[:, 0:n], in_=dmin[:, 0:n], func=FN.Exp, scale=ntemp[:, 0:1])
+            nm = small.tile([P, RING], F32, tag="nmx")
+            nc.vector.tensor_scalar(
+                out=nm[:, 0:n], in0=mx[:, 0:n], scalar1=-1.0, scalar2=None, op0=ALU.mult
+            )
+            nmx[b] = nm
+            rs_t = small.tile([P, RING], F32, tag="rs")
+            rs[b] = rs_t
+            exp1(i0)
+            exp1(i0 + 1)
+            for k in range(n):
+                exp2(i0 + k)
+                if k + 2 < n:
+                    exp1(i0 + k + 2)
+                while done["clamp"] - (i0 + n) < ((k + 1) * AHEAD[b]) // n:
+                    produce()
+                consume(b, k)
+        last = len(BATCHES) - 1
+        for step in range(BATCHES[last], BATCHES[last] + 8):
+            consume(last, step)

@@ -23,7 +23,7 @@ FLOPS = 2 * NODES * S * D * 2
 
 BATCHES = [12, 20, 32, 32, 32]
 RING = 32
-AHEAD = [8, 14, 22, 22, 0]
+AHEAD = [4, 8, 12, 12, 0]
 
 
 def tile_pernodememory_t_kernel(tc, node_fts, data, temp, fixed_lerp, out):
@@ -56,7 +56,8 @@ def tile_pernodememory_t_kernel(tc, node_fts, data, temp, fixed_lerp, out):
         dk = const.tile([P, 2, 4, D], BF16)
         nc.sync.dma_start(out=dk[:], in_=data.rearrange("(g p t) d -> p g t d", g=2, t=4))
         q_sb = const.tile([P, NT, D], BF16)
-        nc.sync.dma_start(out=q_sb[:, 0 : BATCHES[0], :], in_=qv[:, 0 : BATCHES[0], :])
+        nc.sync.dma_start(out=q_sb[:, 0:4, :], in_=qv[:, 0:4, :])
+        nc.sync.dma_start(out=q_sb[:, 4 : BATCHES[0], :], in_=qv[:, 4 : BATCHES[0], :])
         lerp_bf = const.tile([P, 1], BF16)
         nc.scalar.dma_start(out=lerp_bf[:], in_=fixed_lerp.partition_broadcast(P))
         temp_bf = const.tile([P, 1], BF16)
@@ -79,20 +80,19 @@ def tile_pernodememory_t_kernel(tc, node_fts, data, temp, fixed_lerp, out):
             nc.scalar.activation(
                 out=junk[:], in_=dk[:, i // 4, i % 4, :], func=FN.Square, accum_out=m2col[:, i : i + 1]
             )
-        warm = const.tile([P, 1], F32)
-        nc.scalar.activation(out=warm[:], in_=z[:], func=FN.Sqrt)
 
         mt_ps = psq.tile([P, 8, P], BF16, tag="qt")
         for i in range(8):
             nc.tensor.transpose(mt_ps[:, i, :], dk[:, i // 4, i % 4, :], ident_b[:])
         mT2 = const.tile([D, S], BF16)
-        nc.vector.tensor_scalar(
-            out=mT2[:],
-            in0=mt_ps[:].rearrange("d i p -> d (i p)"),
-            scalar1=-2.0,
-            scalar2=None,
-            op0=ALU.mult,
-        )
+        for h in range(2):
+            nc.vector.tensor_scalar(
+                out=mT2[:, HALF * h : HALF * (h + 1)],
+                in0=mt_ps[:, 4 * h : 4 * h + 4, :].rearrange("d i p -> d (i p)"),
+                scalar1=-2.0,
+                scalar2=None,
+                op0=ALU.mult,
+            )
 
         ntemp = const.tile([P, 1], F32)
         lerp = const.tile([P, 1], F32)
@@ -152,11 +152,22 @@ def tile_pernodememory_t_kernel(tc, node_fts, data, temp, fixed_lerp, out):
             qt_sb = qtpool.tile([D, 4, P], BF16, tag="qT")
             nc.vector.tensor_copy(out=qt_sb[:], in_=qt_ps[:])
             qT[quad] = qt_sb
-            sq = sqpool.tile([P, 4, D], F32, tag="sq")
-            nc.gpsimd.tensor_tensor(
-                out=sq[:], in0=q_sb[:, i0 : i0 + 4, :], in1=q_sb[:, i0 : i0 + 4, :], op=ALU.mult
-            )
-            nc.vector.tensor_reduce(out=q2b[b][:, k0 : k0 + 4], in_=sq[:], axis=AX.X, op=ALU.add)
+            if b == 0:
+                for k in range(4):
+                    nc.scalar.activation(
+                        out=junk[:],
+                        in_=q_sb[:, i0 + k, :],
+                        func=FN.Square,
+                        accum_out=q2b[b][:, k0 + k : k0 + k + 1],
+                    )
+            else:
+                sq = sqpool.tile([P, 4, D], F32, tag="sq")
+                nc.gpsimd.tensor_tensor(
+                    out=sq[:], in0=q_sb[:, i0 : i0 + 4, :], in1=q_sb[:, i0 : i0 + 4, :], op=ALU.mult
+                )
+                nc.vector.tensor_reduce(
+                    out=q2b[b][:, k0 : k0 + 4], in_=sq[:], axis=AX.X, op=ALU.add
+                )
             nc.vector.tensor_scalar(
                 out=cb[b][:, k0 : k0 + 4],
                 in0=q2b[b][:, k0 : k0 + 4],
@@ -317,15 +328,20 @@ def tile_pernodememory_t_kernel(tc, node_fts, data, temp, fixed_lerp, out):
                 read_memory((i0 + step - 6) // 4)
             if step >= 3 and (step - 3) % 4 == 0 and step - 3 < n:
                 scale_q((i0 + step - 3) // 4)
-            if 0 <= step - 1 < n:
-                regroup(i0 + step - 1)
             if 0 <= step - 2 < n:
                 quant(i0 + step - 2)
+            if 0 <= step - 1 < n:
+                regroup(i0 + step - 1)
             if step >= 7 and (step - 7) % 4 == 0 and step - 7 < n:
                 finish((i0 + step - 7) // 4)
 
         for quad in range(BATCHES[0] // 4):
             prep(quad)
+            if quad > 0:
+                for k in range(4):
+                    produce()
+        warm = const.tile([P, 1], F32)
+        nc.scalar.activation(out=warm[:], in_=z[:], func=FN.Sqrt)
 
         for b in range(len(BATCHES)):
             i0 = starts[b]
@@ -352,9 +368,7 @@ def tile_pernodememory_t_kernel(tc, node_fts, data, temp, fixed_lerp, out):
             mx = small.tile([P, RING], F32, tag="mx")
             nc.scalar.activation(out=mx[:, 0:n], in_=dmin[:, 0:n], func=FN.Exp, scale=ntemp[:, 0:1])
             nm = small.tile([P, RING], F32, tag="nmx")
-            nc.vector.tensor_scalar(
-                out=nm[:, 0:n], in0=mx[:, 0:n], scalar1=-1.0, scalar2=None, op0=ALU.mult
-            )
+            nc.scalar.mul(out=nm[:, 0:n], in_=mx[:, 0:n], mul=-1.0)
             nmx[b] = nm
             rs_t = small.tile([P, RING], F32, tag="rs")
             rs[b] = rs_t

@@ -23,7 +23,7 @@ FLOPS = 2 * NODES * S * D * 2
 
 BATCHES = [12, 20, 32, 32, 32]
 RING = 32
-AHEAD = [4, 8, 12, 12, 0]
+AHEAD = [6, 10, 16, 16, 0]
 
 
 def tile_pernodememory_t_kernel(tc, node_fts, data, temp, fixed_lerp, out):
@@ -38,8 +38,8 @@ def tile_pernodememory_t_kernel(tc, node_fts, data, temp, fixed_lerp, out):
 
     with ExitStack() as ctx:
         const = ctx.enter_context(tc.tile_pool(name="const", bufs=1))
-        ring = ctx.enter_context(tc.tile_pool(name="ring", bufs=RING))
-        epool = ctx.enter_context(tc.tile_pool(name="epool", bufs=4))
+        ring = ctx.enter_context(tc.tile_pool(name="ring", bufs=RING // 4))
+        epool = ctx.enter_context(tc.tile_pool(name="epool", bufs=2))
         grpool = ctx.enter_context(tc.tile_pool(name="grpool", bufs=3))
         cdpool = ctx.enter_context(tc.tile_pool(name="cdpool", bufs=8))
         qtpool = ctx.enter_context(tc.tile_pool(name="qtpool", bufs=10))
@@ -132,7 +132,7 @@ def tile_pernodememory_t_kernel(tc, node_fts, data, temp, fixed_lerp, out):
         cds = {}
         gps = {}
         qss = {}
-        done = {"prep": 0, "cross": 0, "clamp": 0}
+        done = {"prep": 0, "cross": 0, "clamp": 0, "exp2": 0}
 
         def where(i):
             b = batch_of[i]
@@ -208,10 +208,12 @@ def tile_pernodememory_t_kernel(tc, node_fts, data, temp, fixed_lerp, out):
             if k == 0:
                 um = small.tile([P, RING, 2], F32, tag="umin")
                 umin[b] = um
-            u = ring.tile([P, S], F32, tag="u")
+            if i % 4 == 0:
+                u = ring.tile([P, 4, S], F32, tag="u")
+                us[i // 4] = u
             for h in range(2):
                 nc.vector.tensor_scalar(
-                    out=u[:, HALF * h : HALF * (h + 1)],
+                    out=us[i // 4][:, i % 4, HALF * h : HALF * (h + 1)],
                     in0=xs[i][h][:],
                     scalar1=cb[b][:, k : k + 1],
                     scalar2=None,
@@ -219,7 +221,6 @@ def tile_pernodememory_t_kernel(tc, node_fts, data, temp, fixed_lerp, out):
                     op1=ALU.min,
                     accum_out=umin[b][:, k, h : h + 1],
                 )
-            us[i] = u
             done["clamp"] = i + 1
 
         def produce():
@@ -231,30 +232,34 @@ def tile_pernodememory_t_kernel(tc, node_fts, data, temp, fixed_lerp, out):
 
         def root(i):
             b, k = where(i)
-            nc.scalar.activation(
-                out=us[i][:], in_=us[i][:], func=FN.Sqrt, bias=q2b[b][:, k : k + 1], scale=1.0
-            )
+            u = us[i // 4][:, i % 4, :]
+            nc.scalar.activation(out=u, in_=u, func=FN.Sqrt, bias=q2b[b][:, k : k + 1], scale=1.0)
 
-        def exp1(i):
-            nc.scalar.activation(out=us[i][:], in_=us[i][:], func=FN.Exp, scale=ntemp[:, 0:1])
+        def exp1(quad):
+            u = us[quad][:].rearrange("p k s -> p (k s)")
+            nc.scalar.activation(out=u, in_=u, func=FN.Exp, scale=ntemp[:, 0:1])
 
         def exp2(i):
             b, k = where(i)
-            e = epool.tile([P, S], BF16, tag="e")
+            if i % 4 == 0:
+                e = epool.tile([P, 4, S], BF16, tag="e")
+                es[i // 4] = e
             nc.scalar.activation(
-                out=e[:],
-                in_=us[i][:],
+                out=es[i // 4][:, i % 4, :],
+                in_=us[i // 4][:, i % 4, :],
                 func=FN.Exp,
                 bias=nmx[b][:, k : k + 1],
                 scale=1.0,
                 accum_out=rs[b][:, k : k + 1],
             )
-            es[i] = e
+            done["exp2"] = i + 1
 
         def flip(i):
             et = pse.tile([P, 8, P], BF16, tag="et")
             for c in range(8):
-                nc.tensor.transpose(et[:, c, :], es[i][:, P * c : P * (c + 1)], ident_b[:])
+                nc.tensor.transpose(
+                    et[:, c, :], es[i // 4][:, i % 4, P * c : P * (c + 1)], ident_b[:]
+                )
             ets[i] = et
 
         def regroup(i):
@@ -372,13 +377,15 @@ def tile_pernodememory_t_kernel(tc, node_fts, data, temp, fixed_lerp, out):
             nmx[b] = nm
             rs_t = small.tile([P, RING], F32, tag="rs")
             rs[b] = rs_t
-            exp1(i0)
-            exp1(i0 + 1)
+            exp1(i0 // 4)
             for k in range(n):
+                if k % 4 == 0 and k + 4 < n:
+                    exp1((i0 + k + 4) // 4)
                 exp2(i0 + k)
-                if k + 2 < n:
-                    exp1(i0 + k + 2)
-                while done["clamp"] - (i0 + n) < ((k + 1) * AHEAD[b]) // n:
+                while (
+                    done["clamp"] - (i0 + n) < ((k + 1) * AHEAD[b]) // n
+                    and done["clamp"] - RING + 4 <= done["exp2"]
+                ):
                     produce()
                 consume(b, k)
         last = len(BATCHES) - 1

@@ -24,6 +24,7 @@ FLOPS = 2 * NODES * S * D * 2
 BATCHES = [12, 20, 32, 32, 32]
 RING = 32
 AHEAD = [6, 10, 16, 16, 0]
+SPARE = 3
 
 
 def tile_pernodememory_t_kernel(tc, node_fts, data, temp, fixed_lerp, out):
@@ -38,14 +39,14 @@ def tile_pernodememory_t_kernel(tc, node_fts, data, temp, fixed_lerp, out):
 
     with ExitStack() as ctx:
         const = ctx.enter_context(tc.tile_pool(name="const", bufs=1))
-        ring = ctx.enter_context(tc.tile_pool(name="ring", bufs=RING // 4))
-        epool = ctx.enter_context(tc.tile_pool(name="epool", bufs=2))
+        ring = ctx.enter_context(tc.tile_pool(name="ring", bufs=RING + SPARE))
+        epool = ctx.enter_context(tc.tile_pool(name="epool", bufs=4))
         grpool = ctx.enter_context(tc.tile_pool(name="grpool", bufs=3))
         cdpool = ctx.enter_context(tc.tile_pool(name="cdpool", bufs=8))
         qtpool = ctx.enter_context(tc.tile_pool(name="qtpool", bufs=10))
         sqpool = ctx.enter_context(tc.tile_pool(name="sqpool", bufs=2))
         qspool = ctx.enter_context(tc.tile_pool(name="qspool", bufs=2))
-        obpool = ctx.enter_context(tc.tile_pool(name="obpool", bufs=3))
+        obpool = ctx.enter_context(tc.tile_pool(name="obpool", bufs=2))
         small = ctx.enter_context(tc.tile_pool(name="small", bufs=2))
         psx = ctx.enter_context(tc.psum_pool(name="psx", bufs=4))
         pse = ctx.enter_context(tc.psum_pool(name="pse", bufs=2))
@@ -132,7 +133,7 @@ def tile_pernodememory_t_kernel(tc, node_fts, data, temp, fixed_lerp, out):
         cds = {}
         gps = {}
         qss = {}
-        done = {"prep": 0, "cross": 0, "clamp": 0, "exp2": 0}
+        done = {"prep": 0, "cross": 0, "clamp": 0, "live": 0}
 
         def where(i):
             b = batch_of[i]
@@ -208,12 +209,10 @@ def tile_pernodememory_t_kernel(tc, node_fts, data, temp, fixed_lerp, out):
             if k == 0:
                 um = small.tile([P, RING, 2], F32, tag="umin")
                 umin[b] = um
-            if i % 4 == 0:
-                u = ring.tile([P, 4, S], F32, tag="u")
-                us[i // 4] = u
+            u = ring.tile([P, S], F32, tag="u")
             for h in range(2):
                 nc.vector.tensor_scalar(
-                    out=us[i // 4][:, i % 4, HALF * h : HALF * (h + 1)],
+                    out=u[:, HALF * h : HALF * (h + 1)],
                     in0=xs[i][h][:],
                     scalar1=cb[b][:, k : k + 1],
                     scalar2=None,
@@ -221,7 +220,9 @@ def tile_pernodememory_t_kernel(tc, node_fts, data, temp, fixed_lerp, out):
                     op1=ALU.min,
                     accum_out=umin[b][:, k, h : h + 1],
                 )
+            us[i] = u
             done["clamp"] = i + 1
+            done["live"] = done["live"] + 1
 
         def produce():
             i = done["clamp"]
@@ -232,34 +233,35 @@ def tile_pernodememory_t_kernel(tc, node_fts, data, temp, fixed_lerp, out):
 
         def root(i):
             b, k = where(i)
-            u = us[i // 4][:, i % 4, :]
-            nc.scalar.activation(out=u, in_=u, func=FN.Sqrt, bias=q2b[b][:, k : k + 1], scale=1.0)
+            dist = ring.tile([P, S], F32, tag="u")
+            nc.scalar.activation(
+                out=dist[:], in_=us[i][:], func=FN.Sqrt, bias=q2b[b][:, k : k + 1], scale=1.0
+            )
+            us[i] = dist
 
-        def exp1(quad):
-            u = us[quad][:].rearrange("p k s -> p (k s)")
-            nc.scalar.activation(out=u, in_=u, func=FN.Exp, scale=ntemp[:, 0:1])
+        def exp1(i):
+            sim = ring.tile([P, S], F32, tag="u")
+            nc.scalar.activation(out=sim[:], in_=us[i][:], func=FN.Exp, scale=ntemp[:, 0:1])
+            us[i] = sim
 
         def exp2(i):
             b, k = where(i)
-            if i % 4 == 0:
-                e = epool.tile([P, 4, S], BF16, tag="e")
-                es[i // 4] = e
+            e = epool.tile([P, S], BF16, tag="e")
             nc.scalar.activation(
-                out=es[i // 4][:, i % 4, :],
-                in_=us[i // 4][:, i % 4, :],
+                out=e[:],
+                in_=us[i][:],
                 func=FN.Exp,
                 bias=nmx[b][:, k : k + 1],
                 scale=1.0,
                 accum_out=rs[b][:, k : k + 1],
             )
-            done["exp2"] = i + 1
+            es[i] = e
+            done["live"] = done["live"] - 1
 
         def flip(i):
             et = pse.tile([P, 8, P], BF16, tag="et")
             for c in range(8):
-                nc.tensor.transpose(
-                    et[:, c, :], es[i // 4][:, i % 4, P * c : P * (c + 1)], ident_b[:]
-                )
+                nc.tensor.transpose(et[:, c, :], es[i][:, P * c : P * (c + 1)], ident_b[:])
             ets[i] = et
 
         def regroup(i):
@@ -377,15 +379,13 @@ def tile_pernodememory_t_kernel(tc, node_fts, data, temp, fixed_lerp, out):
             nmx[b] = nm
             rs_t = small.tile([P, RING], F32, tag="rs")
             rs[b] = rs_t
-            exp1(i0 // 4)
+            exp1(i0)
+            exp1(i0 + 1)
             for k in range(n):
-                if k % 4 == 0 and k + 4 < n:
-                    exp1((i0 + k + 4) // 4)
                 exp2(i0 + k)
-                while (
-                    done["clamp"] - (i0 + n) < ((k + 1) * AHEAD[b]) // n
-                    and done["clamp"] - RING + 4 <= done["exp2"]
-                ):
+                if k + 2 < n:
+                    exp1(i0 + k + 2)
+                while done["clamp"] - (i0 + n) < ((k + 1) * AHEAD[b]) // n and done["live"] < RING:
                     produce()
                 consume(b, k)
         last = len(BATCHES) - 1

from contextlib import ExitStack

import concourse.mybir as mybir
from concourse.masks import make_identity

F32 = mybir.dt.float32
BF16 = mybir.dt.bfloat16
U32 = mybir.dt.uint32
U8 = mybir.dt.uint8
FP8X4 = mybir.dt.float8_e4m3fn_x4
ALU = mybir.AluOpType
FN = mybir.ActivationFunctionType
AX = mybir.AxisListType

P = 128
NODES = 32 * 512
S = 1024
D = 128
NT = NODES // P
HALF = 512
EPS = 1e-12
FLOPS = 2 * NODES * S * D * 2

BATCHES = [12, 20, 32, 32, 32]
RING = 32
AHEAD = [6, 10, 16, 16, 0]
SPARE = 3


def tile_pernodememory_t_kernel(tc, node_fts, data, temp, fixed_lerp, out):
    nc = tc.nc
    qv = node_fts.flatten_outer_dims().rearrange("(p t) d -> p t d", t=NT)
    ov = out.flatten_outer_dims().rearrange("(p t) d -> p t d", t=NT)

    starts = [sum(BATCHES[:b]) for b in range(len(BATCHES))]
    batch_of = []
    for b in range(len(BATCHES)):
        batch_of.extend([b] * BATCHES[b])

    with ExitStack() as ctx:
        const = ctx.enter_context(tc.tile_pool(name="const", bufs=1))
        ring = ctx.enter_context(tc.tile_pool(name="ring", bufs=RING + SPARE))
        epool = ctx.enter_context(tc.tile_pool(name="epool", bufs=4))
        grpool = ctx.enter_context(tc.tile_pool(name="grpool", bufs=3))
        cdpool = ctx.enter_context(tc.tile_pool(name="cdpool", bufs=8))
        qtpool = ctx.enter_context(tc.tile_pool(name="qtpool", bufs=10))
        sqpool = ctx.enter_context(tc.tile_pool(name="sqpool", bufs=2))
        qspool = ctx.enter_context(tc.tile_pool(name="qspool", bufs=2))
        obpool = ctx.enter_context(tc.tile_pool(name="obpool", bufs=2))
        small = ctx.enter_context(tc.tile_pool(name="small", bufs=2))
        psx = ctx.enter_context(tc.psum_pool(name="psx", bufs=4))
        pse = ctx.enter_context(tc.psum_pool(name="pse", bufs=2))
        psg = ctx.enter_context(tc.psum_pool(name="psg", bufs=1))
        psq = ctx.enter_context(tc.psum_pool(name="psq", bufs=1))
        ctx.enter_context(tc.manual_schedule())

        dk = const.tile([P, 2, 4, D], BF16)
        nc.sync.dma_start(out=dk[:], in_=data.rearrange("(g p t) d -> p g t d", g=2, t=4))
        q_sb = const.tile([P, NT, D], BF16)
        nc.sync.dma_start(out=q_sb[:, 0:4, :], in_=qv[:, 0:4, :])
        nc.sync.dma_start(out=q_sb[:, 4 : BATCHES[0], :], in_=qv[:, 4 : BATCHES[0], :])
        lerp_bf = const.tile([P, 1], BF16)
        nc.scalar.dma_start(out=lerp_bf[:], in_=fixed_lerp.partition_broadcast(P))
        temp_bf = const.tile([P, 1], BF16)
        nc.scalar.dma_start(out=temp_bf[:], in_=temp.partition_broadcast(P))
        for b in range(1, len(BATCHES)):
            t0 = starts[b]
            t1 = t0 + BATCHES[b]
            nc.sync.dma_start(out=q_sb[:, t0:t1, :], in_=qv[:, t0:t1, :])

        ident_b = const.tile([P, P], BF16)
        make_identity(nc, ident_b[:])
        ident_f = const.tile([P, P], F32)
        make_identity(nc, ident_f[:])

        z = const.tile([P, 1], F32)
        nc.scalar.activation(out=z[:], in_=lerp_bf[:], func=FN.Exp, scale=-1.0)
        m2col = const.tile([P, 8], F32)
        junk = const.tile([P, D], F32)
        for i in range(8):
            nc.scalar.activation(
                out=junk[:], in_=dk[:, i // 4, i % 4, :], func=FN.Square, accum_out=m2col[:, i : i + 1]
            )

        mt_ps = psq.tile([P, 8, P], BF16, tag="qt")
        for i in range(8):
            nc.tensor.transpose(mt_ps[:, i, :], dk[:, i // 4, i % 4, :], ident_b[:])
        mT2 = const.tile([D, S], BF16)
        for h in range(2):
            nc.vector.tensor_scalar(
                out=mT2[:, HALF * h : HALF * (h + 1)],
                in0=mt_ps[:, 4 * h : 4 * h + 4, :].rearrange("d i p -> d (i p)"),
                scalar1=-2.0,
                scalar2=None,
                op0=ALU.mult,
            )

        ntemp = const.tile([P, 1], F32)
        lerp = const.tile([P, 1], F32)
        oml = const.tile([P, 1], F32)
        dcodes = const.tile([P, 2 * D], U32, align_bytes=64)
        dscales = const.tile([P, 2 * D], U8, align_bytes=64)

        def small_constants():
            nc.vector.tensor_scalar(
                out=ntemp[:], in0=temp_bf[:], scalar1=-1.0, scalar2=None, op0=ALU.mult
            )
            den = const.tile([P, 1], F32)
            nc.vector.tensor_scalar(out=den[:], in0=z[:], scalar1=1.0, scalar2=None, op0=ALU.add)
            nc.vector.reciprocal(out=lerp[:], in_=den[:])
            nc.vector.tensor_tensor(out=oml[:], in0=z[:], in1=lerp[:], op=ALU.mult)

        def quantise_data():
            dg = const.tile([P, 2, D, 4], BF16, align_bytes=64)
            nc.vector.tensor_copy(out=dg[:], in_=dk[:].rearrange("p g t d -> p g d t"))
            nc.vector.quantize_mx(
                out=dcodes[:].bitcast(FP8X4),
                scales=dscales[:],
                in_=dg[:].rearrange("p g d t -> p (g d t)"),
            )

        qT = {}
        q2b = {}
        cb = {}
        umin = {}
        nmx = {}
        rs = {}
        xs = {}
        us = {}
        es = {}
        ets = {}
        grs = {}
        cds = {}
        gps = {}
        qss = {}
        done = {"prep": 0, "cross": 0, "clamp": 0, "live": 0}

        def where(i):
            b = batch_of[i]
            return b, i - starts[b]

        def prep(quad):
            i0 = 4 * quad
            b, k0 = where(i0)
            if k0 == 0:
                q2_t = small.tile([P, RING], F32, tag="q2b")
                q2b[b] = q2_t
                c_t = small.tile([P, RING], F32, tag="cb")
                cb[b] = c_t
            qt_ps = psq.tile([P, 4, P], BF16, tag="qt")
            for k in range(4):
                nc.tensor.transpose(qt_ps[:, k, :], q_sb[:, i0 + k, :], ident_b[:])
            qt_sb = qtpool.tile([D, 4, P], BF16, tag="qT")
            nc.vector.tensor_copy(out=qt_sb[:], in_=qt_ps[:])
            qT[quad] = qt_sb
            if b == 0:
                for k in range(4):
                    nc.scalar.activation(
                        out=junk[:],
                        in_=q_sb[:, i0 + k, :],
                        func=FN.Square,
                        accum_out=q2b[b][:, k0 + k : k0 + k + 1],
                    )
            else:
                sq = sqpool.tile([P, 4, D], F32, tag="sq")
                nc.gpsimd.tensor_tensor(
                    out=sq[:], in0=q_sb[:, i0 : i0 + 4, :], in1=q_sb[:, i0 : i0 + 4, :], op=ALU.mult
                )
                nc.vector.tensor_reduce(
                    out=q2b[b][:, k0 : k0 + 4], in_=sq[:], axis=AX.X, op=ALU.add
                )
            nc.vector.tensor_scalar(
                out=cb[b][:, k0 : k0 + 4],
                in0=q2b[b][:, k0 : k0 + 4],
                scalar1=-1.0,
                scalar2=EPS,
                op0=ALU.mult,
                op1=ALU.add,
            )
            done["prep"] = quad + 1

        def cross(i):
            banks = []
            for h in range(2):
                x = psx.tile([P, HALF], F32, tag="x")
                nc.tensor.matmul(
                    out=x[:],
                    lhsT=qT[i // 4][:, i % 4, :],
                    rhs=mT2[:, HALF * h : HALF * (h + 1)],
                    start=True,
                    stop=False,
                )
                for a in range(4):
                    c = 4 * h + a
                    nc.tensor.matmul(
                        out=x[:, P * a : P * (a + 1)],
                        lhsT=m2col[:, c : c + 1].to_broadcast([P, P]),
                        rhs=ident_f[:],
                        is_transpose=True,
                        start=False,
                        stop=(a == 3),
                    )
                banks.append(x)
            xs[i] = banks
            done["cross"] = i + 1

        def clamp(i):
            b, k = where(i)
            if k == 0:
                um = small.tile([P, RING, 2], F32, tag="umin")
                umin[b] = um
            u = ring.tile([P, S], F32, tag="u")
            for h in range(2):
                nc.vector.tensor_scalar(
                    out=u[:, HALF * h : HALF * (h + 1)],
                    in0=xs[i][h][:],
                    scalar1=cb[b][:, k : k + 1],
                    scalar2=None,
                    op0=ALU.max,
                    op1=ALU.min,
                    accum_out=umin[b][:, k, h : h + 1],
                )
            us[i] = u
            done["clamp"] = i + 1
            done["live"] = done["live"] + 1

        def produce():
            i = done["clamp"]
            for j in (i, i + 1):
                if j == done["cross"] and j < NT and j // 4 < done["prep"]:
                    cross(j)
            clamp(i)

        def root(i):
            b, k = where(i)
            dist = ring.tile([P, S], F32, tag="u")
            nc.scalar.activation(
                out=dist[:], in_=us[i][:], func=FN.Sqrt, bias=q2b[b][:, k : k + 1], scale=1.0
            )
            us[i] = dist

        def exp1(i):
            sim = ring.tile([P, S], F32, tag="u")
            nc.scalar.activation(out=sim[:], in_=us[i][:], func=FN.Exp, scale=ntemp[:, 0:1])
            us[i] = sim

        def exp2(i):
            b, k = where(i)
            e = epool.tile([P, S], BF16, tag="e")
            nc.scalar.activation(
                out=e[:],
                in_=us[i][:],
                func=FN.Exp,
                bias=nmx[b][:, k : k + 1],
                scale=1.0,
                accum_out=rs[b][:, k : k + 1],
            )
            es[i] = e
            done["live"] = done["live"] - 1

        def flip(i):
            et = pse.tile([P, 8, P], BF16, tag="et")
            for c in range(8):
                nc.tensor.transpose(et[:, c, :], es[i][:, P * c : P * (c + 1)], ident_b[:])
            ets[i] = et

        def regroup(i):
            gr = grpool.tile([P, S], BF16, tag="gr", align_bytes=64)
            nc.vector.tensor_copy(
                out=gr[:].rearrange("p (g n t) -> p g n t", g=2, t=4),
                in_=ets[i][:].rearrange("p (g t) n -> p g n t", t=4),
            )
            grs[i] = gr

        def quant(i):
            codes = cdpool.tile([P, 2 * P], U32, tag="codes", align_bytes=64)
            scales = cdpool.tile([P, 2 * P], U8, tag="scales", align_bytes=64)
            nc.vector.quantize_mx(out=codes[:].bitcast(FP8X4), scales=scales[:], in_=grs[i][:])
            cds[i] = (codes, scales)

        def read_memory(quad):
            gp = psg.tile([P, 4, D], F32, tag="g")
            for k in range(4):
                codes, scales = cds[4 * quad + k]
                for g in range(2):
                    nc.tensor.matmul_mx(
                        out=gp[:, k, :],
                        lhsT=codes[:, P * g : P * (g + 1)].bitcast(FP8X4),
                        lhsT_scale=scales[:, P * g : P * (g + 1)],
                        rhs=dcodes[:, D * g : D * (g + 1)].bitcast(FP8X4),
                        rhs_scale=dscales[:, D * g : D * (g + 1)],
                        start=(g == 0),
                        stop=(g == 1),
                    )
            gps[quad] = gp

        def scale_q(quad):
            qs = qspool.tile([P, 4, D], F32, tag="qs")
            nc.gpsimd.tensor_scalar(
                out=qs[:],
                in0=q_sb[:, 4 * quad : 4 * quad + 4, :],
                scalar1=oml[:, 0:1],
                scalar2=0.0,
                op0=ALU.mult,
                op1=ALU.add,
            )
            qss[quad] = qs

        def finish(quad):
            b, k0 = where(4 * quad)
            ra = small.tile([P, 4], F32, tag="ra")
            nc.vector.reciprocal(out=ra[:], in_=rs[b][:, k0 : k0 + 4])
            wgt = small.tile([P, 4], F32, tag="wgt")
            nc.vector.tensor_scalar(
                out=wgt[:], in0=ra[:], scalar1=lerp[:, 0:1], scalar2=None, op0=ALU.mult
            )
            ob = obpool.tile([P, 4, D], F32, tag="ob")
            for k in range(4):
                nc.vector.scalar_tensor_tensor(
                    out=ob[:, k, :],
                    in0=gps[quad][:, k, :],
                    scalar=wgt[:, k : k + 1],
                    in1=qss[quad][:, k, :],
                    op0=ALU.mult,
                    op1=ALU.add,
                )
            nc.sync.dma_start(out=ov[:, 4 * quad : 4 * quad + 4, :], in_=ob[:])

        def consume(b, step):
            i0 = starts[b]
            n = BATCHES[b]
            if 0 <= step - 1 < n:
                flip(i0 + step - 1)
            if step >= 6 and (step - 6) % 4 == 0 and step - 6 < n:
                read_memory((i0 + step - 6) // 4)
            if step >= 3 and (step - 3) % 4 == 0 and step - 3 < n:
                scale_q((i0 + step - 3) // 4)
            if 0 <= step - 2 < n:
                quant(i0 + step - 2)
            if 0 <= step - 1 < n:
                regroup(i0 + step - 1)
            if step >= 7 and (step - 7) % 4 == 0 and step - 7 < n:
                finish((i0 + step - 7) // 4)

        for quad in range(BATCHES[0] // 4):
            prep(quad)
            if quad > 0:
                for k in range(4):
                    produce()
        warm = const.tile([P, 1], F32)
        nc.scalar.activation(out=warm[:], in_=z[:], func=FN.Sqrt)

        for b in range(len(BATCHES)):
            i0 = starts[b]
            n = BATCHES[b]
            if b > 0:
                for step in range(BATCHES[b - 1], BATCHES[b - 1] + 8):
                    consume(b - 1, step)
            while done["clamp"] < i0 + n:
                produce()
            dmin = small.tile([P, RING], F32, tag="dmin")
            nc.vector.tensor_reduce(out=dmin[:, 0:n], in_=umin[b][:, 0:n, :], axis=AX.X, op=ALU.min)
            nc.vector.tensor_tensor(
                out=dmin[:, 0:n], in0=dmin[:, 0:n], in1=q2b[b][:, 0:n], op=ALU.add
            )
            if b == 0:
                small_constants()
                quantise_data()
            if b + 1 < len(BATCHES):
                for quad in range(starts[b + 1] // 4, (starts[b + 1] + BATCHES[b + 1]) // 4):
                    prep(quad)
            for k in range(n):
                root(i0 + k)
            nc.scalar.activation(out=dmin[:, 0:n], in_=dmin[:, 0:n], func=FN.Sqrt)
            mx = small.tile([P, RING], F32, tag="mx")
            nc.scalar.activation(out=mx[:, 0:n], in_=dmin[:, 0:n], func=FN.Exp, scale=ntemp[:, 0:1])
            nm = small.tile([P, RING], F32, tag="nmx")
            nc.scalar.mul(out=nm[:, 0:n], in_=mx[:, 0:n], mul=-1.0)
            nmx[b] = nm
            rs_t = small.tile([P, RING], F32, tag="rs")
            rs[b] = rs_t
            exp1(i0)
            exp1(i0 + 1)
            for k in range(n):
                exp2(i0 + k)
                if k + 2 < n:
                    exp1(i0 + k + 2)
                while done["clamp"] - (i0 + n) < ((k + 1) * AHEAD[b]) // n and done["live"] < RING:
                    produce()
                consume(b, k)
        last = len(BATCHES) - 1
        for step in range(BATCHES[last], BATCHES[last] + 8):
            consume(last, step)
